import numpy as np
import ml_dtypes

BF16 = ml_dtypes.bfloat16


def bf(x):
    return np.asarray(x, np.float32).astype(BF16)


def f32(x):
    return np.asarray(x, np.float32)


def f64(x):
    return np.asarray(x).astype(np.float64)


def striped(idx):
    return np.tile(idx.reshape(-1, 16).T, (8, 1))


C, S, N = 512, 2048, 256


def setup_inputs():
    return {"emb": f32(np.random.standard_normal((C, S))), "pos": f32(np.random.standard_normal((C, N))), "keep": f32(np.random.random((1, N)) < 0.5), "wout": bf(np.random.standard_normal((C, S)) / np.sqrt(C)), "bout": f32(0.1 * np.random.standard_normal((S, 1))), "offs": striped(np.random.permutation(np.tile(np.arange(S), 2))[:N])}


def reference(emb, pos, keep, wout, bout, offs):
    idx = offs[:16].T.reshape(-1)
    h = f64(emb)[:, idx] + f64(pos) * f64(keep)
    return f64(wout).T @ h + f64(bout)

@@ -1,0 +1,64 @@
+import concourse.mybir as mybir
+
+F32 = mybir.dt.float32
+BF16 = mybir.dt.bfloat16
+U16 = mybir.dt.uint16
+ADD = mybir.AluOpType.add
+MULT = mybir.AluOpType.mult
+COPY = mybir.ActivationFunctionType.Copy
+IDENTITY = mybir.ActivationFunctionType.Identity
+
+C, S, N = 512, 2048, 256
+P = 128
+CB = C // P
+VB = S // P
+STORE = 4
+
+FLOPS = 2 * C * S * N
+
+
+def tile_transformerdecoder_kernel(tc, emb, pos, keep, wout, bout, offs, out):
+    nc = tc.nc
+    out_rows = out.rearrange("(p b) j -> p b j", b=VB)
+    bout_rows = bout.rearrange("(p b) o -> p (b o)", b=VB)
+
+    with tc.tile_pool(name="held", bufs=1) as held, tc.psum_pool(name="psum", bufs=8) as psum:
+        offsets = held.tile([P, N // 16], U16, name="offsets")
+        nc.sync.dma_start(offsets[:], offs)
+        keep_all = held.tile([P, N], F32, name="keep_all")
+        nc.sync.dma_start(keep_all[:], keep.rearrange("o j -> (o j)").partition_broadcast(P))
+        bias = held.tile([P, VB], F32, name="bias")
+        nc.sync.dma_start(bias[:], bout_rows)
+
+        pos_sb, emb_sb, wout_sb = [], [], []
+        for k in range(CB):
+            rows = slice(k * P, (k + 1) * P)
+            pos_sb.append(held.tile([P, N], F32, name=f"pos{k}"))
+            nc.sync.dma_start(pos_sb[k][:], pos[rows, :])
+            emb_sb.append(held.tile([P, S], F32, name=f"emb{k}"))
+            nc.sync.dma_start(emb_sb[k][:], emb[rows, :])
+            wout_sb.append(held.tile([P, S], BF16, name=f"wout{k}"))
+            nc.sync.dma_start(wout_sb[k][:], wout[rows, :])
+
+        h_bf = []
+        for k in range(CB):
+            masked = held.tile([P, N], F32, name=f"masked{k}")
+            nc.vector.tensor_tensor(masked[:], pos_sb[k][:], keep_all[:], MULT)
+            h_f32 = held.tile([P, N], F32, name=f"h_f32_{k}")
+            nc.vector.tensor_tensor(h_f32[:], emb_sb[k][:].indirect(offsets[:]), masked[:], ADD)
+            h_bf.append(held.tile([P, N], BF16, name=f"h_bf{k}"))
+            nc.scalar.activation(h_bf[k][:], h_f32[:], COPY)
+
+        logits = held.tile([P, VB, N], F32, name="logits")
+        for b in range(VB):
+            acc = psum.tile([P, N], F32, name="acc")
+            for k in range(CB):
+                weights = wout_sb[k][:].rearrange("c (p b) -> c b p", b=VB)[:, b, :]
+                nc.tensor.matmul(acc[:], weights, h_bf[k][:], start=(k == 0), stop=(k == CB - 1))
+            if b % 2 == 0:
+                nc.vector.tensor_scalar(logits[:, b, :], acc[:], bias[:, b : b + 1], None, ADD)
+            else:
+                nc.scalar.activation(logits[:, b, :], acc[:], IDENTITY, bias=bias[:, b : b + 1])
+            if b % STORE == STORE - 1:
+                done = slice(b + 1 - STORE, b + 1)
+                nc.sync.dma_start(out_rows[:, done, :], logits[:, done, :])

@@ -12,6 +12,8 @@ C, S, N = 512, 2048, 256
 P = 128
 CB = C // P
 VB = S // P
+BANKS = 8
+PER_BANK = VB // BANKS
 STORE = 4
 
 FLOPS = 2 * C * S * N
@@ -22,43 +24,49 @@ def tile_transformerdecoder_kernel(tc, emb, pos, keep, wout, bout, offs, out):
     out_rows = out.rearrange("(p b) j -> p b j", b=VB)
     bout_rows = bout.rearrange("(p b) o -> p (b o)", b=VB)
 
-    with tc.tile_pool(name="held", bufs=1) as held, tc.psum_pool(name="psum", bufs=8) as psum:
+    with tc.tile_pool(name="held", bufs=1) as held, tc.psum_pool(name="psum", bufs=1) as psum:
         offsets = held.tile([P, N // 16], U16, name="offsets")
         nc.sync.dma_start(offsets[:], offs)
         keep_all = held.tile([P, N], F32, name="keep_all")
         nc.sync.dma_start(keep_all[:], keep.rearrange("o j -> (o j)").partition_broadcast(P))
         bias = held.tile([P, VB], F32, name="bias")
         nc.sync.dma_start(bias[:], bout_rows)
+        pos_sb = held.tile([P, CB, N], F32, name="pos_sb")
+        nc.sync.dma_start(pos_sb[:], pos.rearrange("(k p) j -> p k j", p=P))
 
-        pos_sb, emb_sb, wout_sb = [], [], []
+        emb_sb, wout_sb = [], []
         for k in range(CB):
             rows = slice(k * P, (k + 1) * P)
-            pos_sb.append(held.tile([P, N], F32, name=f"pos{k}"))
-            nc.sync.dma_start(pos_sb[k][:], pos[rows, :])
-            emb_sb.append(held.tile([P, S], F32, name=f"emb{k}"))
-            nc.sync.dma_start(emb_sb[k][:], emb[rows, :])
             wout_sb.append(held.tile([P, S], BF16, name=f"wout{k}"))
             nc.sync.dma_start(wout_sb[k][:], wout[rows, :])
+            emb_sb.append(held.tile([P, S], F32, name=f"emb{k}"))
+            nc.sync.dma_start(emb_sb[k][:], emb[rows, :])
 
-        h_bf = []
+        banks = [psum.tile([P, PER_BANK, N], F32, name=f"bank{i}") for i in range(BANKS)]
         for k in range(CB):
             masked = held.tile([P, N], F32, name=f"masked{k}")
-            nc.vector.tensor_tensor(masked[:], pos_sb[k][:], keep_all[:], MULT)
+            nc.vector.tensor_tensor(masked[:], pos_sb[:, k, :], keep_all[:], MULT)
             h_f32 = held.tile([P, N], F32, name=f"h_f32_{k}")
             nc.vector.tensor_tensor(h_f32[:], emb_sb[k][:].indirect(offsets[:]), masked[:], ADD)
-            h_bf.append(held.tile([P, N], BF16, name=f"h_bf{k}"))
-            nc.scalar.activation(h_bf[k][:], h_f32[:], COPY)
+            h_bf = held.tile([P, N], BF16, name=f"h_bf{k}")
+            nc.scalar.activation(h_bf[:], h_f32[:], COPY)
+            for b in range(VB):
+                weights = wout_sb[k][:].rearrange("c (p b) -> c b p", b=VB)[:, b, :]
+                nc.tensor.matmul(
+                    banks[b // PER_BANK][:, b % PER_BANK, :],
+                    weights,
+                    h_bf[:],
+                    start=(k == 0 and b % PER_BANK == 0),
+                    stop=(k == CB - 1 and b % PER_BANK == PER_BANK - 1),
+                )
 
         logits = held.tile([P, VB, N], F32, name="logits")
         for b in range(VB):
-            acc = psum.tile([P, N], F32, name="acc")
-            for k in range(CB):
-                weights = wout_sb[k][:].rearrange("c (p b) -> c b p", b=VB)[:, b, :]
-                nc.tensor.matmul(acc[:], weights, h_bf[k][:], start=(k == 0), stop=(k == CB - 1))
-            if b % 2 == 0:
-                nc.vector.tensor_scalar(logits[:, b, :], acc[:], bias[:, b : b + 1], None, ADD)
+            summed = banks[b // PER_BANK][:, b % PER_BANK, :]
+            if (b // PER_BANK) % 2 == 0:
+                nc.vector.tensor_scalar(logits[:, b, :], summed, bias[:, b : b + 1], None, ADD)
             else:
-                nc.scalar.activation(logits[:, b, :], acc[:], IDENTITY, bias=bias[:, b : b + 1])
+                nc.scalar.activation(logits[:, b, :], summed, IDENTITY, bias=bias[:, b : b + 1])
             if b % STORE == STORE - 1:
                 done = slice(b + 1 - STORE, b + 1)
                 nc.sync.dma_start(out_rows[:, done, :], logits[:, done, :])

@@ -21,8 +21,8 @@ FLOPS = 2 * C * S * N
 
 def tile_transformerdecoder_kernel(tc, emb, pos, keep, wout, bout, offs, out):
     nc = tc.nc
-    out_rows = out.rearrange("(p b) j -> p b j", b=VB)
-    bout_rows = bout.rearrange("(p b) o -> p (b o)", b=VB)
+    out_rows = out.rearrange("(b p) j -> p b j", p=P)
+    bout_rows = bout.rearrange("(b p) o -> p (b o)", p=P)
 
     with tc.tile_pool(name="held", bufs=1) as held, tc.psum_pool(name="psum", bufs=1) as psum:
         offsets = held.tile([P, N // 16], U16, name="offsets")
@@ -30,7 +30,8 @@ def tile_transformerdecoder_kernel(tc, emb, pos, keep, wout, bout, offs, out):
         keep_all = held.tile([P, N], F32, name="keep_all")
         nc.sync.dma_start(keep_all[:], keep.rearrange("o j -> (o j)").partition_broadcast(P))
         bias = held.tile([P, VB], F32, name="bias")
-        nc.sync.dma_start(bias[:], bout_rows)
+        with nc.allow_non_contiguous_dma(reason="the bias, one value a partition and step"):
+            nc.sync.dma_start(bias[:], bout_rows)
         pos_sb = held.tile([P, CB, N], F32, name="pos_sb")
         nc.sync.dma_start(pos_sb[:], pos.rearrange("(k p) j -> p k j", p=P))
 
@@ -51,7 +52,7 @@ def tile_transformerdecoder_kernel(tc, emb, pos, keep, wout, bout, offs, out):
             h_bf = held.tile([P, N], BF16, name=f"h_bf{k}")
             nc.scalar.activation(h_bf[:], h_f32[:], COPY)
             for b in range(VB):
-                weights = wout_sb[k][:].rearrange("c (p b) -> c b p", b=VB)[:, b, :]
+                weights = wout_sb[k][:, b * P : (b + 1) * P]
                 nc.tensor.matmul(
                     banks[b // PER_BANK][:, b % PER_BANK, :],
                     weights,

@@ -14,15 +14,14 @@ CB = C // P
 VB = S // P
 BANKS = 8
 PER_BANK = VB // BANKS
-STORE = 4
 
 FLOPS = 2 * C * S * N
 
 
 def tile_transformerdecoder_kernel(tc, emb, pos, keep, wout, bout, offs, out):
     nc = tc.nc
-    out_rows = out.rearrange("(b p) j -> p b j", p=P)
-    bout_rows = bout.rearrange("(b p) o -> p (b o)", p=P)
+    out_rows = out.rearrange("(p b) j -> p b j", b=VB)
+    bout_rows = bout.rearrange("(p b) o -> p (b o)", b=VB)
 
     with tc.tile_pool(name="held", bufs=1) as held, tc.psum_pool(name="psum", bufs=1) as psum:
         offsets = held.tile([P, N // 16], U16, name="offsets")
@@ -30,29 +29,28 @@ def tile_transformerdecoder_kernel(tc, emb, pos, keep, wout, bout, offs, out):
         keep_all = held.tile([P, N], F32, name="keep_all")
         nc.sync.dma_start(keep_all[:], keep.rearrange("o j -> (o j)").partition_broadcast(P))
         bias = held.tile([P, VB], F32, name="bias")
-        with nc.allow_non_contiguous_dma(reason="the bias, one value a partition and step"):
-            nc.sync.dma_start(bias[:], bout_rows)
-        pos_sb = held.tile([P, CB, N], F32, name="pos_sb")
-        nc.sync.dma_start(pos_sb[:], pos.rearrange("(k p) j -> p k j", p=P))
+        nc.sync.dma_start(bias[:], bout_rows)
 
-        emb_sb, wout_sb = [], []
+        pos_sb, emb_sb, wout_sb = [], [], []
         for k in range(CB):
             rows = slice(k * P, (k + 1) * P)
-            wout_sb.append(held.tile([P, S], BF16, name=f"wout{k}"))
-            nc.sync.dma_start(wout_sb[k][:], wout[rows, :])
+            pos_sb.append(held.tile([P, N], F32, name=f"pos{k}"))
+            nc.sync.dma_start(pos_sb[k][:], pos[rows, :])
             emb_sb.append(held.tile([P, S], F32, name=f"emb{k}"))
             nc.sync.dma_start(emb_sb[k][:], emb[rows, :])
+            wout_sb.append(held.tile([P, S], BF16, name=f"wout{k}"))
+            nc.sync.dma_start(wout_sb[k][:], wout[rows, :])
 
         banks = [psum.tile([P, PER_BANK, N], F32, name=f"bank{i}") for i in range(BANKS)]
         for k in range(CB):
             masked = held.tile([P, N], F32, name=f"masked{k}")
-            nc.vector.tensor_tensor(masked[:], pos_sb[:, k, :], keep_all[:], MULT)
+            nc.vector.tensor_tensor(masked[:], pos_sb[k][:], keep_all[:], MULT)
             h_f32 = held.tile([P, N], F32, name=f"h_f32_{k}")
             nc.vector.tensor_tensor(h_f32[:], emb_sb[k][:].indirect(offsets[:]), masked[:], ADD)
             h_bf = held.tile([P, N], BF16, name=f"h_bf{k}")
             nc.scalar.activation(h_bf[:], h_f32[:], COPY)
             for b in range(VB):
-                weights = wout_sb[k][:, b * P : (b + 1) * P]
+                weights = wout_sb[k][:].rearrange("c (p b) -> c b p", b=VB)[:, b, :]
                 nc.tensor.matmul(
                     banks[b // PER_BANK][:, b % PER_BANK, :],
                     weights,
@@ -62,12 +60,13 @@ def tile_transformerdecoder_kernel(tc, emb, pos, keep, wout, bout, offs, out):
                 )
 
         logits = held.tile([P, VB, N], F32, name="logits")
-        for b in range(VB):
-            summed = banks[b // PER_BANK][:, b % PER_BANK, :]
-            if (b // PER_BANK) % 2 == 0:
-                nc.vector.tensor_scalar(logits[:, b, :], summed, bias[:, b : b + 1], None, ADD)
-            else:
-                nc.scalar.activation(logits[:, b, :], summed, IDENTITY, bias=bias[:, b : b + 1])
-            if b % STORE == STORE - 1:
-                done = slice(b + 1 - STORE, b + 1)
-                nc.sync.dma_start(out_rows[:, done, :], logits[:, done, :])
+        for i in range(BANKS):
+            first = i * PER_BANK
+            for b in range(first, first + PER_BANK):
+                summed = banks[i][:, b - first, :]
+                if i % 2 == 0:
+                    nc.vector.tensor_scalar(logits[:, b, :], summed, bias[:, b : b + 1], None, ADD)
+                else:
+                    nc.scalar.activation(logits[:, b, :], summed, IDENTITY, bias=bias[:, b : b + 1])
+            steps = slice(first, first + PER_BANK)
+            nc.sync.dma_start(out_rows[:, steps, :], logits[:, steps, :])

@@ -5,7 +5,6 @@ BF16 = mybir.dt.bfloat16
 U16 = mybir.dt.uint16
 ADD = mybir.AluOpType.add
 MULT = mybir.AluOpType.mult
-COPY = mybir.ActivationFunctionType.Copy
 IDENTITY = mybir.ActivationFunctionType.Identity
 
 C, S, N = 512, 2048, 256
@@ -48,7 +47,7 @@ def tile_transformerdecoder_kernel(tc, emb, pos, keep, wout, bout, offs, out):
             h_f32 = held.tile([P, N], F32, name=f"h_f32_{k}")
             nc.vector.tensor_tensor(h_f32[:], emb_sb[k][:].indirect(offsets[:]), masked[:], ADD)
             h_bf = held.tile([P, N], BF16, name=f"h_bf{k}")
-            nc.scalar.activation(h_bf[:], h_f32[:], COPY)
+            nc.vector.tensor_copy(h_bf[:], h_f32[:])
             for b in range(VB):
                 weights = wout_sb[k][:].rearrange("c (p b) -> c b p", b=VB)[:, b, :]
                 nc.tensor.matmul(

@@ -19,6 +19,9 @@ FLOPS = 2 * C * S * N
 
 def tile_transformerdecoder_kernel(tc, emb, pos, keep, wout, bout, offs, out):
     nc = tc.nc
+    pos_blocks = pos.rearrange("(p k) j -> p k j", k=CB)
+    emb_blocks = emb.rearrange("(p k) s -> p k s", k=CB)
+    wout_blocks = wout.rearrange("(p k) v -> p k v", k=CB)
     out_rows = out.rearrange("(p b) j -> p b j", b=VB)
     bout_rows = bout.rearrange("(p b) o -> p (b o)", b=VB)
 
@@ -30,26 +33,31 @@ def tile_transformerdecoder_kernel(tc, emb, pos, keep, wout, bout, offs, out):
         bias = held.tile([P, VB], F32, name="bias")
         nc.sync.dma_start(bias[:], bout_rows)
 
-        pos_sb, emb_sb, wout_sb = [], [], []
-        for k in range(CB):
-            rows = slice(k * P, (k + 1) * P)
-            pos_sb.append(held.tile([P, N], F32, name=f"pos{k}"))
-            nc.sync.dma_start(pos_sb[k][:], pos[rows, :])
-            emb_sb.append(held.tile([P, S], F32, name=f"emb{k}"))
-            nc.sync.dma_start(emb_sb[k][:], emb[rows, :])
-            wout_sb.append(held.tile([P, S], BF16, name=f"wout{k}"))
-            nc.sync.dma_start(wout_sb[k][:], wout[rows, :])
+        pos_sb = held.tile([P, CB, N], F32, name="pos_sb")
+        emb_sb = [held.tile([P, S], F32, name=f"emb{k}") for k in range(CB)]
+        wout_01 = held.tile([P, 2, S], BF16, name="wout_01")
+        wout_2 = held.tile([P, S], BF16, name="wout_2")
+        wout_3 = held.tile([P, S], BF16, name="wout_3")
+        nc.sync.dma_start(pos_sb[:], pos_blocks)
+        nc.sync.dma_start(emb_sb[0][:], emb_blocks[:, 0, :])
+        nc.sync.dma_start(wout_01[:], wout_blocks[:, 0:2, :])
+        nc.sync.dma_start(emb_sb[1][:], emb_blocks[:, 1, :])
+        nc.sync.dma_start(emb_sb[2][:], emb_blocks[:, 2, :])
+        nc.sync.dma_start(wout_2[:], wout_blocks[:, 2, :])
+        nc.sync.dma_start(emb_sb[3][:], emb_blocks[:, 3, :])
+        nc.sync.dma_start(wout_3[:], wout_blocks[:, 3, :])
+        wout_sb = [wout_01[:, 0, :], wout_01[:, 1, :], wout_2[:], wout_3[:]]
 
         banks = [psum.tile([P, PER_BANK, N], F32, name=f"bank{i}") for i in range(BANKS)]
         for k in range(CB):
             masked = held.tile([P, N], F32, name=f"masked{k}")
-            nc.vector.tensor_tensor(masked[:], pos_sb[k][:], keep_all[:], MULT)
+            nc.vector.tensor_tensor(masked[:], pos_sb[:, k, :], keep_all[:], MULT)
             h_f32 = held.tile([P, N], F32, name=f"h_f32_{k}")
             nc.vector.tensor_tensor(h_f32[:], emb_sb[k][:].indirect(offsets[:]), masked[:], ADD)
             h_bf = held.tile([P, N], BF16, name=f"h_bf{k}")
             nc.vector.tensor_copy(h_bf[:], h_f32[:])
             for b in range(VB):
-                weights = wout_sb[k][:].rearrange("c (p b) -> c b p", b=VB)[:, b, :]
+                weights = wout_sb[k].rearrange("c (p b) -> c b p", b=VB)[:, b, :]
                 nc.tensor.matmul(
                     banks[b // PER_BANK][:, b % PER_BANK, :],
                     weights,
@@ -60,12 +68,16 @@ def tile_transformerdecoder_kernel(tc, emb, pos, keep, wout, bout, offs, out):
 
         logits = held.tile([P, VB, N], F32, name="logits")
         for i in range(BANKS):
-            first = i * PER_BANK
-            for b in range(first, first + PER_BANK):
-                summed = banks[i][:, b - first, :]
+            for b in range(i * PER_BANK, (i + 1) * PER_BANK):
+                summed = banks[i][:, b % PER_BANK, :]
                 if i % 2 == 0:
                     nc.vector.tensor_scalar(logits[:, b, :], summed, bias[:, b : b + 1], None, ADD)
                 else:
                     nc.scalar.activation(logits[:, b, :], summed, IDENTITY, bias=bias[:, b : b + 1])
-            steps = slice(first, first + PER_BANK)
+
+        stored = 0
+        while stored < BANKS:
+            count = max(stored, 1)
+            steps = slice(stored * PER_BANK, (stored + count) * PER_BANK)
             nc.sync.dma_start(out_rows[:, steps, :], logits[:, steps, :])
+            stored += count

@@ -13,6 +13,8 @@ CB = C // P
 VB = S // P
 BANKS = 8
 PER_BANK = VB // BANKS
+HALF = S // 2
+ROWS = VB // 2
 
 FLOPS = 2 * C * S * N
 
@@ -22,62 +24,82 @@ def tile_transformerdecoder_kernel(tc, emb, pos, keep, wout, bout, offs, out):
     pos_blocks = pos.rearrange("(p k) j -> p k j", k=CB)
     emb_blocks = emb.rearrange("(p k) s -> p k s", k=CB)
     wout_blocks = wout.rearrange("(p k) v -> p k v", k=CB)
-    out_rows = out.rearrange("(p b) j -> p b j", b=VB)
-    bout_rows = bout.rearrange("(p b) o -> p (b o)", b=VB)
+    out_rows = out.rearrange("(h p r) j -> p h r j", h=2, r=ROWS)
+    bout_rows = bout.rearrange("(h p r) o -> p h (r o)", h=2, r=ROWS)
 
     with tc.tile_pool(name="held", bufs=1) as held, tc.psum_pool(name="psum", bufs=1) as psum:
         offsets = held.tile([P, N // 16], U16, name="offsets")
         nc.sync.dma_start(offsets[:], offs)
         keep_all = held.tile([P, N], F32, name="keep_all")
         nc.sync.dma_start(keep_all[:], keep.rearrange("o j -> (o j)").partition_broadcast(P))
-        bias = held.tile([P, VB], F32, name="bias")
-        nc.sync.dma_start(bias[:], bout_rows)
 
         pos_sb = held.tile([P, CB, N], F32, name="pos_sb")
         emb_sb = [held.tile([P, S], F32, name=f"emb{k}") for k in range(CB)]
         wout_01 = held.tile([P, 2, S], BF16, name="wout_01")
-        wout_2 = held.tile([P, S], BF16, name="wout_2")
-        wout_3 = held.tile([P, S], BF16, name="wout_3")
+        wout_2_first = held.tile([P, HALF], BF16, name="wout_2_first")
+        wout_3_first = held.tile([P, HALF], BF16, name="wout_3_first")
+        wout_23_second = held.tile([P, 2, HALF], BF16, name="wout_23_second")
+        bias = held.tile([P, 2, ROWS], F32, name="bias")
         nc.sync.dma_start(pos_sb[:], pos_blocks)
         nc.sync.dma_start(emb_sb[0][:], emb_blocks[:, 0, :])
         nc.sync.dma_start(wout_01[:], wout_blocks[:, 0:2, :])
         nc.sync.dma_start(emb_sb[1][:], emb_blocks[:, 1, :])
         nc.sync.dma_start(emb_sb[2][:], emb_blocks[:, 2, :])
-        nc.sync.dma_start(wout_2[:], wout_blocks[:, 2, :])
+        nc.sync.dma_start(wout_2_first[:], wout_blocks[:, 2, 0:HALF])
         nc.sync.dma_start(emb_sb[3][:], emb_blocks[:, 3, :])
-        nc.sync.dma_start(wout_3[:], wout_blocks[:, 3, :])
-        wout_sb = [wout_01[:, 0, :], wout_01[:, 1, :], wout_2[:], wout_3[:]]
+        nc.sync.dma_start(wout_3_first[:], wout_blocks[:, 3, 0:HALF])
+        nc.sync.dma_start(bias[:], bout_rows)
+        nc.sync.dma_start(wout_23_second[:], wout_blocks[:, 2:4, HALF:S])
+        wout_sb = [
+            [wout_01[:, 0, 0:HALF], wout_01[:, 0, HALF:S]],
+            [wout_01[:, 1, 0:HALF], wout_01[:, 1, HALF:S]],
+            [wout_2_first[:], wout_23_second[:, 0, :]],
+            [wout_3_first[:], wout_23_second[:, 1, :]],
+        ]
 
-        banks = [psum.tile([P, PER_BANK, N], F32, name=f"bank{i}") for i in range(BANKS)]
+        h_bf = []
         for k in range(CB):
             masked = held.tile([P, N], F32, name=f"masked{k}")
             nc.vector.tensor_tensor(masked[:], pos_sb[:, k, :], keep_all[:], MULT)
             h_f32 = held.tile([P, N], F32, name=f"h_f32_{k}")
             nc.vector.tensor_tensor(h_f32[:], emb_sb[k][:].indirect(offsets[:]), masked[:], ADD)
-            h_bf = held.tile([P, N], BF16, name=f"h_bf{k}")
-            nc.vector.tensor_copy(h_bf[:], h_f32[:])
-            for b in range(VB):
-                weights = wout_sb[k].rearrange("c (p b) -> c b p", b=VB)[:, b, :]
-                nc.tensor.matmul(
-                    banks[b // PER_BANK][:, b % PER_BANK, :],
-                    weights,
-                    h_bf[:],
-                    start=(k == 0 and b % PER_BANK == 0),
-                    stop=(k == CB - 1 and b % PER_BANK == PER_BANK - 1),
-                )
+            h_bf.append(held.tile([P, N], BF16, name=f"h_bf{k}"))
+            nc.vector.tensor_copy(h_bf[k][:], h_f32[:])
+
+        banks = [psum.tile([P, PER_BANK, N], F32, name=f"bank{i}") for i in range(BANKS)]
+
+        def multiply(k, step):
+            half, r = divmod(step, ROWS)
+            weights = wout_sb[k][half].rearrange("c (p r) -> c r p", r=ROWS)
+            nc.tensor.matmul(
+                banks[step // PER_BANK][:, step % PER_BANK, :],
+                weights[:, r, :],
+                h_bf[k][:],
+                start=(k == 0 and step % PER_BANK == 0),
+                stop=(k == CB - 1 and step % PER_BANK == PER_BANK - 1),
+            )
+
+        for k in range(2):
+            for step in range(VB):
+                multiply(k, step)
+        for step in range(ROWS):
+            multiply(2, step)
+        for i in range(BANKS):
+            for k in (3,) if i < BANKS // 2 else (2, 3):
+                for step in range(i * PER_BANK, (i + 1) * PER_BANK):
+                    multiply(k, step)
 
         logits = held.tile([P, VB, N], F32, name="logits")
         for i in range(BANKS):
-            for b in range(i * PER_BANK, (i + 1) * PER_BANK):
-                summed = banks[i][:, b % PER_BANK, :]
+            for step in range(i * PER_BANK, (i + 1) * PER_BANK):
+                summed = banks[i][:, step % PER_BANK, :]
+                bias_col = bias[:, step // ROWS, step % ROWS : step % ROWS + 1]
                 if i % 2 == 0:
-                    nc.vector.tensor_scalar(logits[:, b, :], summed, bias[:, b : b + 1], None, ADD)
+                    nc.vector.tensor_scalar(logits[:, step, :], summed, bias_col, None, ADD)
                 else:
-                    nc.scalar.activation(logits[:, b, :], summed, IDENTITY, bias=bias[:, b : b + 1])
+                    nc.scalar.activation(logits[:, step, :], summed, IDENTITY, bias=bias_col)
 
-        stored = 0
-        while stored < BANKS:
-            count = max(stored, 1)
-            steps = slice(stored * PER_BANK, (stored + count) * PER_BANK)
-            nc.sync.dma_start(out_rows[:, steps, :], logits[:, steps, :])
-            stored += count
+        for first, count in ((0, 1), (1, 1), (2, 2), (4, 2), (6, 2)):
+            half, r = divmod(first * PER_BANK, ROWS)
+            steps = slice(first * PER_BANK, (first + count) * PER_BANK)
+            nc.sync.dma_start(out_rows[:, half, r : r + count * PER_BANK, :], logits[:, steps, :])

@@ -32,6 +32,8 @@ def tile_transformerdecoder_kernel(tc, emb, pos, keep, wout, bout, offs, out):
         nc.sync.dma_start(offsets[:], offs)
         keep_all = held.tile([P, N], F32, name="keep_all")
         nc.sync.dma_start(keep_all[:], keep.rearrange("o j -> (o j)").partition_broadcast(P))
+        bias = held.tile([P, 2, ROWS], F32, name="bias")
+        nc.sync.dma_start(bias[:], bout_rows)
 
         pos_sb = held.tile([P, CB, N], F32, name="pos_sb")
         emb_sb = [held.tile([P, S], F32, name=f"emb{k}") for k in range(CB)]
@@ -39,7 +41,6 @@ def tile_transformerdecoder_kernel(tc, emb, pos, keep, wout, bout, offs, out):
         wout_2_first = held.tile([P, HALF], BF16, name="wout_2_first")
         wout_3_first = held.tile([P, HALF], BF16, name="wout_3_first")
         wout_23_second = held.tile([P, 2, HALF], BF16, name="wout_23_second")
-        bias = held.tile([P, 2, ROWS], F32, name="bias")
         nc.sync.dma_start(pos_sb[:], pos_blocks)
         nc.sync.dma_start(emb_sb[0][:], emb_blocks[:, 0, :])
         nc.sync.dma_start(wout_01[:], wout_blocks[:, 0:2, :])
@@ -48,7 +49,6 @@ def tile_transformerdecoder_kernel(tc, emb, pos, keep, wout, bout, offs, out):
         nc.sync.dma_start(wout_2_first[:], wout_blocks[:, 2, 0:HALF])
         nc.sync.dma_start(emb_sb[3][:], emb_blocks[:, 3, :])
         nc.sync.dma_start(wout_3_first[:], wout_blocks[:, 3, 0:HALF])
-        nc.sync.dma_start(bias[:], bout_rows)
         nc.sync.dma_start(wout_23_second[:], wout_blocks[:, 2:4, HALF:S])
         wout_sb = [
             [wout_01[:, 0, 0:HALF], wout_01[:, 0, HALF:S]],

@@ -30,8 +30,10 @@ def tile_transformerdecoder_kernel(tc, emb, pos, keep, wout, bout, offs, out):
     with tc.tile_pool(name="held", bufs=1) as held, tc.psum_pool(name="psum", bufs=1) as psum:
         offsets = held.tile([P, N // 16], U16, name="offsets")
         nc.sync.dma_start(offsets[:], offs)
-        keep_all = held.tile([P, N], F32, name="keep_all")
-        nc.sync.dma_start(keep_all[:], keep.rearrange("o j -> (o j)").partition_broadcast(P))
+        keep_row = held.tile([P, N], F32, name="keep_row")
+        nc.vector.memset(keep_row[:], 0.0)
+        ones = held.tile([P, P], F32, name="ones")
+        nc.gpsimd.memset(ones[:], 1.0)
         bias = held.tile([P, 2, ROWS], F32, name="bias")
         nc.sync.dma_start(bias[:], bout_rows)
 
@@ -42,6 +44,7 @@ def tile_transformerdecoder_kernel(tc, emb, pos, keep, wout, bout, offs, out):
         wout_3_first = held.tile([P, HALF], BF16, name="wout_3_first")
         wout_23_second = held.tile([P, 2, HALF], BF16, name="wout_23_second")
         nc.sync.dma_start(pos_sb[:], pos_blocks)
+        nc.sync.dma_start(keep_row[0:1, :], keep)
         nc.sync.dma_start(emb_sb[0][:], emb_blocks[:, 0, :])
         nc.sync.dma_start(wout_01[:], wout_blocks[:, 0:2, :])
         nc.sync.dma_start(emb_sb[1][:], emb_blocks[:, 1, :])
@@ -57,16 +60,22 @@ def tile_transformerdecoder_kernel(tc, emb, pos, keep, wout, bout, offs, out):
             [wout_3_first[:], wout_23_second[:, 1, :]],
         ]
 
+        banks = [psum.tile([P, PER_BANK, N], F32, name=f"bank{i}") for i in range(BANKS)]
+
+        keep_all = banks[BANKS - 1][:, 0, :]
+        nc.tensor.matmul(keep_all, ones[:], keep_row[:], start=True, stop=True)
+
+        masked = [held.tile([P, N], F32, name=f"masked{k}") for k in range(CB)]
+        for k in range(CB):
+            nc.vector.tensor_tensor(masked[k][:], pos_sb[:, k, :], keep_all, MULT)
+
         h_bf = []
         for k in range(CB):
-            masked = held.tile([P, N], F32, name=f"masked{k}")
-            nc.vector.tensor_tensor(masked[:], pos_sb[:, k, :], keep_all[:], MULT)
             h_f32 = held.tile([P, N], F32, name=f"h_f32_{k}")
-            nc.vector.tensor_tensor(h_f32[:], emb_sb[k][:].indirect(offsets[:]), masked[:], ADD)
+            nc.vector.tensor_tensor(h_f32[:], emb_sb[k][:].indirect(offsets[:]), masked[k][:], ADD)
             h_bf.append(held.tile([P, N], BF16, name=f"h_bf{k}"))
             nc.vector.tensor_copy(h_bf[k][:], h_f32[:])
 
-        banks = [psum.tile([P, PER_BANK, N], F32, name=f"bank{i}") for i in range(BANKS)]
 
         def multiply(k, step):
             half, r = divmod(step, ROWS)
@@ -99,7 +108,7 @@ def tile_transformerdecoder_kernel(tc, emb, pos, keep, wout, bout, offs, out):
                 else:
                     nc.scalar.activation(logits[:, step, :], summed, IDENTITY, bias=bias_col)
 
-        for first, count in ((0, 1), (1, 1), (2, 2), (4, 2), (6, 2)):
+        for first, count in ((0, 1), (1, 1), (2, 2), (4, 2), (6, 1), (7, 1)):
             half, r = divmod(first * PER_BANK, ROWS)
             steps = slice(first * PER_BANK, (first + count) * PER_BANK)
             nc.sync.dma_start(out_rows[:, half, r : r + count * PER_BANK, :], logits[:, steps, :])

@@ -40,24 +40,21 @@ def tile_transformerdecoder_kernel(tc, emb, pos, keep, wout, bout, offs, out):
         pos_sb = held.tile([P, CB, N], F32, name="pos_sb")
         emb_sb = [held.tile([P, S], F32, name=f"emb{k}") for k in range(CB)]
         wout_01 = held.tile([P, 2, S], BF16, name="wout_01")
-        wout_2_first = held.tile([P, HALF], BF16, name="wout_2_first")
-        wout_3_first = held.tile([P, HALF], BF16, name="wout_3_first")
-        wout_23_second = held.tile([P, 2, HALF], BF16, name="wout_23_second")
+        wout_late = [[held.tile([P, HALF], BF16, name=f"wout_{k}_{half}") for half in range(2)] for k in (2, 3)]
         nc.sync.dma_start(pos_sb[:], pos_blocks)
         nc.sync.dma_start(keep_row[0:1, :], keep)
         nc.sync.dma_start(emb_sb[0][:], emb_blocks[:, 0, :])
         nc.sync.dma_start(wout_01[:], wout_blocks[:, 0:2, :])
-        nc.sync.dma_start(emb_sb[1][:], emb_blocks[:, 1, :])
-        nc.sync.dma_start(emb_sb[2][:], emb_blocks[:, 2, :])
-        nc.sync.dma_start(wout_2_first[:], wout_blocks[:, 2, 0:HALF])
-        nc.sync.dma_start(emb_sb[3][:], emb_blocks[:, 3, :])
-        nc.sync.dma_start(wout_3_first[:], wout_blocks[:, 3, 0:HALF])
-        nc.sync.dma_start(wout_23_second[:], wout_blocks[:, 2:4, HALF:S])
+        for k in range(1, CB):
+            nc.sync.dma_start(emb_sb[k][:], emb_blocks[:, k, :])
+        for half in range(2):
+            for k in (2, 3):
+                nc.sync.dma_start(wout_late[k - 2][half][:], wout_blocks[:, k, half * HALF : (half + 1) * HALF])
         wout_sb = [
             [wout_01[:, 0, 0:HALF], wout_01[:, 0, HALF:S]],
             [wout_01[:, 1, 0:HALF], wout_01[:, 1, HALF:S]],
-            [wout_2_first[:], wout_23_second[:, 0, :]],
-            [wout_3_first[:], wout_23_second[:, 1, :]],
+            [wout_late[0][0][:], wout_late[0][1][:]],
+            [wout_late[1][0][:], wout_late[1][1][:]],
         ]
 
         banks = [psum.tile([P, PER_BANK, N], F32, name=f"bank{i}") for i in range(BANKS)]
@@ -88,15 +85,18 @@ def tile_transformerdecoder_kernel(tc, emb, pos, keep, wout, bout, offs, out):
                 stop=(k == CB - 1 and step % PER_BANK == PER_BANK - 1),
             )
 
-        for k in range(2):
-            for step in range(VB):
+        def multiply_bank(k, i):
+            for step in range(i * PER_BANK, (i + 1) * PER_BANK):
                 multiply(k, step)
-        for step in range(ROWS):
-            multiply(2, step)
+
+        for k in range(2):
+            for i in range(BANKS):
+                multiply_bank(k, i)
+        multiply_bank(2, 0)
         for i in range(BANKS):
-            for k in (3,) if i < BANKS // 2 else (2, 3):
-                for step in range(i * PER_BANK, (i + 1) * PER_BANK):
-                    multiply(k, step)
+            if i + 1 < BANKS:
+                multiply_bank(2, i + 1)
+            multiply_bank(3, i)
 
         logits = held.tile([P, VB, N], F32, name="logits")
         for i in range(BANKS):

@@ -108,7 +108,7 @@ def tile_transformerdecoder_kernel(tc, emb, pos, keep, wout, bout, offs, out):
                 else:
                     nc.scalar.activation(logits[:, step, :], summed, IDENTITY, bias=bias_col)
 
-        for first, count in ((0, 1), (1, 1), (2, 2), (4, 2), (6, 1), (7, 1)):
-            half, r = divmod(first * PER_BANK, ROWS)
-            steps = slice(first * PER_BANK, (first + count) * PER_BANK)
-            nc.sync.dma_start(out_rows[:, half, r : r + count * PER_BANK, :], logits[:, steps, :])
+        for i in range(BANKS):
+            half, r = divmod(i * PER_BANK, ROWS)
+            steps = slice(i * PER_BANK, (i + 1) * PER_BANK)
+            nc.sync.dma_start(out_rows[:, half, r : r + PER_BANK, :], logits[:, steps, :])

@@ -35,7 +35,6 @@ def tile_transformerdecoder_kernel(tc, emb, pos, keep, wout, bout, offs, out):
         ones = held.tile([P, P], F32, name="ones")
         nc.gpsimd.memset(ones[:], 1.0)
         bias = held.tile([P, 2, ROWS], F32, name="bias")
-        nc.sync.dma_start(bias[:], bout_rows)
 
         pos_sb = held.tile([P, CB, N], F32, name="pos_sb")
         emb_sb = [held.tile([P, S], F32, name=f"emb{k}") for k in range(CB)]
@@ -50,6 +49,8 @@ def tile_transformerdecoder_kernel(tc, emb, pos, keep, wout, bout, offs, out):
         for half in range(2):
             for k in (2, 3):
                 nc.sync.dma_start(wout_late[k - 2][half][:], wout_blocks[:, k, half * HALF : (half + 1) * HALF])
+            if half == 0:
+                nc.sync.dma_start(bias[:], bout_rows)
         wout_sb = [
             [wout_01[:, 0, 0:HALF], wout_01[:, 0, HALF:S]],
             [wout_01[:, 1, 0:HALF], wout_01[:, 1, HALF:S]],
@@ -71,7 +72,10 @@ def tile_transformerdecoder_kernel(tc, emb, pos, keep, wout, bout, offs, out):
             h_f32 = held.tile([P, N], F32, name=f"h_f32_{k}")
             nc.vector.tensor_tensor(h_f32[:], emb_sb[k][:].indirect(offsets[:]), masked[k][:], ADD)
             h_bf.append(held.tile([P, N], BF16, name=f"h_bf{k}"))
-            nc.vector.tensor_copy(h_bf[k][:], h_f32[:])
+            if k < CB - 1:
+                nc.scalar.copy(h_bf[k][:], h_f32[:])
+            else:
+                nc.vector.tensor_copy(h_bf[k][:], h_f32[:])
 
 
         def multiply(k, step):
@@ -110,5 +114,9 @@ def tile_transformerdecoder_kernel(tc, emb, pos, keep, wout, bout, offs, out):
 
         for i in range(BANKS):
             half, r = divmod(i * PER_BANK, ROWS)
-            steps = slice(i * PER_BANK, (i + 1) * PER_BANK)
-            nc.sync.dma_start(out_rows[:, half, r : r + PER_BANK, :], logits[:, steps, :])
+            if i in (0, BANKS - 1):
+                for s in range(PER_BANK):
+                    nc.sync.dma_start(out_rows[:, half, r + s, :], logits[:, i * PER_BANK + s, :])
+            else:
+                steps = slice(i * PER_BANK, (i + 1) * PER_BANK)
+                nc.sync.dma_start(out_rows[:, half, r : r + PER_BANK, :], logits[:, steps, :])

@@ -1,4 +1,5 @@
 import concourse.mybir as mybir
+from concourse.masks import make_identity
 
 F32 = mybir.dt.float32
 BF16 = mybir.dt.bfloat16
@@ -14,7 +15,7 @@ VB = S // P
 BANKS = 8
 PER_BANK = VB // BANKS
 HALF = S // 2
-ROWS = VB // 2
+HALF_BANKS = BANKS // 2
 
 FLOPS = 2 * C * S * N
 
@@ -24,8 +25,8 @@ def tile_transformerdecoder_kernel(tc, emb, pos, keep, wout, bout, offs, out):
     pos_blocks = pos.rearrange("(p k) j -> p k j", k=CB)
     emb_blocks = emb.rearrange("(p k) s -> p k s", k=CB)
     wout_blocks = wout.rearrange("(p k) v -> p k v", k=CB)
-    out_rows = out.rearrange("(h p r) j -> p h r j", h=2, r=ROWS)
-    bout_rows = bout.rearrange("(h p r) o -> p h (r o)", h=2, r=ROWS)
+    out_banks = out.rearrange("(i p s) j -> p i s j", i=BANKS, s=PER_BANK)
+    bout_banks = bout.rearrange("(i x) o -> i (x o)", i=BANKS)
 
     with tc.tile_pool(name="held", bufs=1) as held, tc.psum_pool(name="psum", bufs=1) as psum:
         offsets = held.tile([P, N // 16], U16, name="offsets")
@@ -34,7 +35,10 @@ def tile_transformerdecoder_kernel(tc, emb, pos, keep, wout, bout, offs, out):
         nc.vector.memset(keep_row[:], 0.0)
         ones = held.tile([P, P], F32, name="ones")
         nc.gpsimd.memset(ones[:], 1.0)
-        bias = held.tile([P, 2, ROWS], F32, name="bias")
+        bias_rows = held.tile([P, PER_BANK * P], F32, name="bias_rows")
+        nc.vector.memset(bias_rows[:], 0.0)
+        identity = held.tile([P, P], F32, name="identity")
+        make_identity(nc, identity[:])
 
         pos_sb = held.tile([P, CB, N], F32, name="pos_sb")
         emb_sb = [held.tile([P, S], F32, name=f"emb{k}") for k in range(CB)]
@@ -42,6 +46,7 @@ def tile_transformerdecoder_kernel(tc, emb, pos, keep, wout, bout, offs, out):
         wout_late = [[held.tile([P, HALF], BF16, name=f"wout_{k}_{half}") for half in range(2)] for k in (2, 3)]
         nc.sync.dma_start(pos_sb[:], pos_blocks)
         nc.sync.dma_start(keep_row[0:1, :], keep)
+        nc.sync.dma_start(bias_rows[0:BANKS, :], bout_banks)
         nc.sync.dma_start(emb_sb[0][:], emb_blocks[:, 0, :])
         nc.sync.dma_start(wout_01[:], wout_blocks[:, 0:2, :])
         for k in range(1, CB):
@@ -49,8 +54,6 @@ def tile_transformerdecoder_kernel(tc, emb, pos, keep, wout, bout, offs, out):
         for half in range(2):
             for k in (2, 3):
                 nc.sync.dma_start(wout_late[k - 2][half][:], wout_blocks[:, k, half * HALF : (half + 1) * HALF])
-            if half == 0:
-                nc.sync.dma_start(bias[:], bout_rows)
         wout_sb = [
             [wout_01[:, 0, 0:HALF], wout_01[:, 0, HALF:S]],
             [wout_01[:, 1, 0:HALF], wout_01[:, 1, HALF:S]],
@@ -62,6 +65,18 @@ def tile_transformerdecoder_kernel(tc, emb, pos, keep, wout, bout, offs, out):
 
         keep_all = banks[BANKS - 1][:, 0, :]
         nc.tensor.matmul(keep_all, ones[:], keep_row[:], start=True, stop=True)
+
+        bias = held.tile([P, VB], F32, name="bias")
+        bias_turned = banks[BANKS - 1][:, 1, 0:VB]
+        for s in range(PER_BANK):
+            nc.tensor.matmul(
+                bias_turned[:, s * BANKS : (s + 1) * BANKS],
+                bias_rows[:].rearrange("i (p s) -> i s p", s=PER_BANK)[:, s, :],
+                identity[:, 0:BANKS],
+                start=True,
+                stop=True,
+            )
+        nc.vector.tensor_copy(bias[:], bias_turned)
 
         masked = [held.tile([P, N], F32, name=f"masked{k}") for k in range(CB)]
         for k in range(CB):
@@ -79,11 +94,11 @@ def tile_transformerdecoder_kernel(tc, emb, pos, keep, wout, bout, offs, out):
 
 
         def multiply(k, step):
-            half, r = divmod(step, ROWS)
-            weights = wout_sb[k][half].rearrange("c (p r) -> c r p", r=ROWS)
+            i, s = divmod(step, PER_BANK)
+            weights = wout_sb[k][i // HALF_BANKS].rearrange("c (i p s) -> c i s p", i=HALF_BANKS, s=PER_BANK)
             nc.tensor.matmul(
-                banks[step // PER_BANK][:, step % PER_BANK, :],
-                weights[:, r, :],
+                banks[i][:, s, :],
+                weights[:, i % HALF_BANKS, s, :],
                 h_bf[k][:],
                 start=(k == 0 and step % PER_BANK == 0),
                 stop=(k == CB - 1 and step % PER_BANK == PER_BANK - 1),
@@ -104,19 +119,17 @@ def tile_transformerdecoder_kernel(tc, emb, pos, keep, wout, bout, offs, out):
 
         logits = held.tile([P, VB, N], F32, name="logits")
         for i in range(BANKS):
-            for step in range(i * PER_BANK, (i + 1) * PER_BANK):
-                summed = banks[i][:, step % PER_BANK, :]
-                bias_col = bias[:, step // ROWS, step % ROWS : step % ROWS + 1]
+            for s in range(PER_BANK):
+                step = i * PER_BANK + s
+                bias_col = bias[:, s * BANKS + i : s * BANKS + i + 1]
                 if i % 2 == 0:
-                    nc.vector.tensor_scalar(logits[:, step, :], summed, bias_col, None, ADD)
+                    nc.vector.tensor_scalar(logits[:, step, :], banks[i][:, s, :], bias_col, None, ADD)
                 else:
-                    nc.scalar.activation(logits[:, step, :], summed, IDENTITY, bias=bias_col)
+                    nc.scalar.activation(logits[:, step, :], banks[i][:, s, :], IDENTITY, bias=bias_col)
 
         for i in range(BANKS):
-            half, r = divmod(i * PER_BANK, ROWS)
             if i in (0, BANKS - 1):
                 for s in range(PER_BANK):
-                    nc.sync.dma_start(out_rows[:, half, r + s, :], logits[:, i * PER_BANK + s, :])
+                    nc.sync.dma_start(out_banks[:, i, s, :], logits[:, i * PER_BANK + s, :])
             else:
-                steps = slice(i * PER_BANK, (i + 1) * PER_BANK)
-                nc.sync.dma_start(out_rows[:, half, r : r + PER_BANK, :], logits[:, steps, :])
+                nc.sync.dma_start(out_banks[:, i, :, :], logits[:, i * PER_BANK : (i + 1) * PER_BANK, :])

@@ -14,8 +14,8 @@ CB = C // P
 VB = S // P
 BANKS = 8
 PER_BANK = VB // BANKS
-HALF = S // 2
-HALF_BANKS = BANKS // 2
+BANK_ROWS = PER_BANK * P
+AHEAD = 2
 
 FLOPS = 2 * C * S * N
 
@@ -43,7 +43,14 @@ def tile_transformerdecoder_kernel(tc, emb, pos, keep, wout, bout, offs, out):
         pos_sb = held.tile([P, CB, N], F32, name="pos_sb")
         emb_sb = [held.tile([P, S], F32, name=f"emb{k}") for k in range(CB)]
         wout_01 = held.tile([P, 2, S], BF16, name="wout_01")
-        wout_late = [[held.tile([P, HALF], BF16, name=f"wout_{k}_{half}") for half in range(2)] for k in (2, 3)]
+        wout_late = [
+            [held.tile([P, AHEAD * BANK_ROWS], BF16, name=f"wout_{k}_{g}") for g in range(BANKS // AHEAD)] for k in (2, 3)
+        ]
+
+        def load_late(k, g):
+            columns = slice(g * AHEAD * BANK_ROWS, (g + 1) * AHEAD * BANK_ROWS)
+            nc.sync.dma_start(wout_late[k - 2][g][:], wout_blocks[:, k, columns])
+
         nc.sync.dma_start(pos_sb[:], pos_blocks)
         nc.sync.dma_start(keep_row[0:1, :], keep)
         nc.sync.dma_start(bias_rows[0:BANKS, :], bout_banks)
@@ -51,15 +58,16 @@ def tile_transformerdecoder_kernel(tc, emb, pos, keep, wout, bout, offs, out):
         nc.sync.dma_start(wout_01[:], wout_blocks[:, 0:2, :])
         for k in range(1, CB):
             nc.sync.dma_start(emb_sb[k][:], emb_blocks[:, k, :])
-        for half in range(2):
-            for k in (2, 3):
-                nc.sync.dma_start(wout_late[k - 2][half][:], wout_blocks[:, k, half * HALF : (half + 1) * HALF])
-        wout_sb = [
-            [wout_01[:, 0, 0:HALF], wout_01[:, 0, HALF:S]],
-            [wout_01[:, 1, 0:HALF], wout_01[:, 1, HALF:S]],
-            [wout_late[0][0][:], wout_late[0][1][:]],
-            [wout_late[1][0][:], wout_late[1][1][:]],
-        ]
+        load_late(2, 0)
+        for g in range(BANKS // AHEAD):
+            if g + 1 < BANKS // AHEAD:
+                load_late(2, g + 1)
+            load_late(3, g)
+
+        def bank_weights(k, i):
+            if k < 2:
+                return wout_01[:, k, i * BANK_ROWS : (i + 1) * BANK_ROWS]
+            return wout_late[k - 2][i // AHEAD][:, (i % AHEAD) * BANK_ROWS : (i % AHEAD + 1) * BANK_ROWS]
 
         banks = [psum.tile([P, PER_BANK, N], F32, name=f"bank{i}") for i in range(BANKS)]
 
@@ -95,10 +103,10 @@ def tile_transformerdecoder_kernel(tc, emb, pos, keep, wout, bout, offs, out):
 
         def multiply(k, step):
             i, s = divmod(step, PER_BANK)
-            weights = wout_sb[k][i // HALF_BANKS].rearrange("c (i p s) -> c i s p", i=HALF_BANKS, s=PER_BANK)
+            weights = bank_weights(k, i).rearrange("c (p s) -> c s p", s=PER_BANK)
             nc.tensor.matmul(
                 banks[i][:, s, :],
-                weights[:, i % HALF_BANKS, s, :],
+                weights[:, s, :],
                 h_bf[k][:],
                 start=(k == 0 and step % PER_BANK == 0),
                 stop=(k == CB - 1 and step % PER_BANK == PER_BANK - 1),
@@ -111,10 +119,11 @@ def tile_transformerdecoder_kernel(tc, emb, pos, keep, wout, bout, offs, out):
         for k in range(2):
             for i in range(BANKS):
                 multiply_bank(k, i)
-        multiply_bank(2, 0)
+        for i in range(AHEAD):
+            multiply_bank(2, i)
         for i in range(BANKS):
-            if i + 1 < BANKS:
-                multiply_bank(2, i + 1)
+            if i + AHEAD < BANKS:
+                multiply_bank(2, i + AHEAD)
             multiply_bank(3, i)
 
         logits = held.tile([P, VB, N], F32, name="logits")

@@ -15,7 +15,9 @@ VB = S // P
 BANKS = 8
 PER_BANK = VB // BANKS
 BANK_ROWS = PER_BANK * P
-AHEAD = 2
+GROUP = 2
+GROUPS = BANKS // GROUP
+LEAD = 3
 
 FLOPS = 2 * C * S * N
 
@@ -43,12 +45,10 @@ def tile_transformerdecoder_kernel(tc, emb, pos, keep, wout, bout, offs, out):
         pos_sb = held.tile([P, CB, N], F32, name="pos_sb")
         emb_sb = [held.tile([P, S], F32, name=f"emb{k}") for k in range(CB)]
         wout_01 = held.tile([P, 2, S], BF16, name="wout_01")
-        wout_late = [
-            [held.tile([P, AHEAD * BANK_ROWS], BF16, name=f"wout_{k}_{g}") for g in range(BANKS // AHEAD)] for k in (2, 3)
-        ]
+        wout_late = [[held.tile([P, GROUP * BANK_ROWS], BF16, name=f"wout_{k}_{g}") for g in range(GROUPS)] for k in (2, 3)]
 
         def load_late(k, g):
-            columns = slice(g * AHEAD * BANK_ROWS, (g + 1) * AHEAD * BANK_ROWS)
+            columns = slice(g * GROUP * BANK_ROWS, (g + 1) * GROUP * BANK_ROWS)
             nc.sync.dma_start(wout_late[k - 2][g][:], wout_blocks[:, k, columns])
 
         nc.sync.dma_start(pos_sb[:], pos_blocks)
@@ -58,16 +58,18 @@ def tile_transformerdecoder_kernel(tc, emb, pos, keep, wout, bout, offs, out):
         nc.sync.dma_start(wout_01[:], wout_blocks[:, 0:2, :])
         for k in range(1, CB):
             nc.sync.dma_start(emb_sb[k][:], emb_blocks[:, k, :])
-        load_late(2, 0)
-        for g in range(BANKS // AHEAD):
-            if g + 1 < BANKS // AHEAD:
-                load_late(2, g + 1)
+        lead_groups = (LEAD + GROUP - 1) // GROUP
+        for g in range(lead_groups):
+            load_late(2, g)
+        for g in range(GROUPS):
+            if g >= lead_groups:
+                load_late(2, g)
             load_late(3, g)
 
         def bank_weights(k, i):
             if k < 2:
                 return wout_01[:, k, i * BANK_ROWS : (i + 1) * BANK_ROWS]
-            return wout_late[k - 2][i // AHEAD][:, (i % AHEAD) * BANK_ROWS : (i % AHEAD + 1) * BANK_ROWS]
+            return wout_late[k - 2][i // GROUP][:, (i % GROUP) * BANK_ROWS : (i % GROUP + 1) * BANK_ROWS]
 
         banks = [psum.tile([P, PER_BANK, N], F32, name=f"bank{i}") for i in range(BANKS)]
 
@@ -119,11 +121,11 @@ def tile_transformerdecoder_kernel(tc, emb, pos, keep, wout, bout, offs, out):
         for k in range(2):
             for i in range(BANKS):
                 multiply_bank(k, i)
-        for i in range(AHEAD):
+        for i in range(LEAD):
             multiply_bank(2, i)
         for i in range(BANKS):
-            if i + AHEAD < BANKS:
-                multiply_bank(2, i + AHEAD)
+            if i >= LEAD:
+                multiply_bank(2, i)
             multiply_bank(3, i)
 
         logits = held.tile([P, VB, N], F32, name="logits")

@@ -97,7 +97,7 @@ def tile_transformerdecoder_kernel(tc, emb, pos, keep, wout, bout, offs, out):
             h_f32 = held.tile([P, N], F32, name=f"h_f32_{k}")
             nc.vector.tensor_tensor(h_f32[:], emb_sb[k][:].indirect(offsets[:]), masked[k][:], ADD)
             h_bf.append(held.tile([P, N], BF16, name=f"h_bf{k}"))
-            if k < CB - 1:
+            if k == 0:
                 nc.scalar.copy(h_bf[k][:], h_f32[:])
             else:
                 nc.vector.tensor_copy(h_bf[k][:], h_f32[:])

import concourse.mybir as mybir
from concourse.masks import make_identity

F32 = mybir.dt.float32
BF16 = mybir.dt.bfloat16
U16 = mybir.dt.uint16
ADD = mybir.AluOpType.add
MULT = mybir.AluOpType.mult
IDENTITY = mybir.ActivationFunctionType.Identity

C, S, N = 512, 2048, 256
P = 128
CB = C // P
VB = S // P
BANKS = 8
PER_BANK = VB // BANKS
BANK_ROWS = PER_BANK * P
GROUP = 2
GROUPS = BANKS // GROUP
LEAD = 3

FLOPS = 2 * C * S * N


def tile_transformerdecoder_kernel(tc, emb, pos, keep, wout, bout, offs, out):
    nc = tc.nc
    pos_blocks = pos.rearrange("(p k) j -> p k j", k=CB)
    emb_blocks = emb.rearrange("(p k) s -> p k s", k=CB)
    wout_blocks = wout.rearrange("(p k) v -> p k v", k=CB)
    out_banks = out.rearrange("(i p s) j -> p i s j", i=BANKS, s=PER_BANK)
    bout_banks = bout.rearrange("(i x) o -> i (x o)", i=BANKS)

    with tc.tile_pool(name="held", bufs=1) as held, tc.psum_pool(name="psum", bufs=1) as psum:
        offsets = held.tile([P, N // 16], U16, name="offsets")
        nc.sync.dma_start(offsets[:], offs)
        keep_row = held.tile([P, N], F32, name="keep_row")
        nc.vector.memset(keep_row[:], 0.0)
        ones = held.tile([P, P], F32, name="ones")
        nc.gpsimd.memset(ones[:], 1.0)
        bias_rows = held.tile([P, PER_BANK * P], F32, name="bias_rows")
        nc.vector.memset(bias_rows[:], 0.0)
        identity = held.tile([P, P], F32, name="identity")
        make_identity(nc, identity[:])

        pos_sb = held.tile([P, CB, N], F32, name="pos_sb")
        emb_sb = [held.tile([P, S], F32, name=f"emb{k}") for k in range(CB)]
        wout_01 = held.tile([P, 2, S], BF16, name="wout_01")
        wout_late = [[held.tile([P, GROUP * BANK_ROWS], BF16, name=f"wout_{k}_{g}") for g in range(GROUPS)] for k in (2, 3)]

        def load_late(k, g):
            columns = slice(g * GROUP * BANK_ROWS, (g + 1) * GROUP * BANK_ROWS)
            nc.sync.dma_start(wout_late[k - 2][g][:], wout_blocks[:, k, columns])

        nc.sync.dma_start(pos_sb[:], pos_blocks)
        nc.sync.dma_start(keep_row[0:1, :], keep)
        nc.sync.dma_start(bias_rows[0:BANKS, :], bout_banks)
        nc.sync.dma_start(emb_sb[0][:], emb_blocks[:, 0, :])
        nc.sync.dma_start(wout_01[:], wout_blocks[:, 0:2, :])
        for k in range(1, CB):
            nc.sync.dma_start(emb_sb[k][:], emb_blocks[:, k, :])
        lead_groups = (LEAD + GROUP - 1) // GROUP
        for g in range(lead_groups):
            load_late(2, g)
        for g in range(GROUPS):
            if g >= lead_groups:
                load_late(2, g)
            load_late(3, g)

        def bank_weights(k, i):
            if k < 2:
                return wout_01[:, k, i * BANK_ROWS : (i + 1) * BANK_ROWS]
            return wout_late[k - 2][i // GROUP][:, (i % GROUP) * BANK_ROWS : (i % GROUP + 1) * BANK_ROWS]

        banks = [psum.tile([P, PER_BANK, N], F32, name=f"bank{i}") for i in range(BANKS)]

        keep_all = banks[BANKS - 1][:, 0, :]
        nc.tensor.matmul(keep_all, ones[:], keep_row[:], start=True, stop=True)

        bias = held.tile([P, VB], F32, name="bias")
        bias_turned = banks[BANKS - 1][:, 1, 0:VB]
        for s in range(PER_BANK):
            nc.tensor.matmul(
                bias_turned[:, s * BANKS : (s + 1) * BANKS],
                bias_rows[:].rearrange("i (p s) -> i s p", s=PER_BANK)[:, s, :],
                identity[:, 0:BANKS],
                start=True,
                stop=True,
            )
        nc.vector.tensor_copy(bias[:], bias_turned)

        masked = [held.tile([P, N], F32, name=f"masked{k}") for k in range(CB)]
        for k in range(CB):
            nc.vector.tensor_tensor(masked[k][:], pos_sb[:, k, :], keep_all, MULT)

        h_bf = []
        for k in range(CB):
            h_f32 = held.tile([P, N], F32, name=f"h_f32_{k}")
            nc.vector.tensor_tensor(h_f32[:], emb_sb[k][:].indirect(offsets[:]), masked[k][:], ADD)
            h_bf.append(held.tile([P, N], BF16, name=f"h_bf{k}"))
            if k == 0:
                nc.scalar.copy(h_bf[k][:], h_f32[:])
            else:
                nc.vector.tensor_copy(h_bf[k][:], h_f32[:])


        def multiply(k, step):
            i, s = divmod(step, PER_BANK)
            weights = bank_weights(k, i).rearrange("c (p s) -> c s p", s=PER_BANK)
            nc.tensor.matmul(
                banks[i][:, s, :],
                weights[:, s, :],
                h_bf[k][:],
                start=(k == 0 and step % PER_BANK == 0),
                stop=(k == CB - 1 and step % PER_BANK == PER_BANK - 1),
            )

        def multiply_bank(k, i):
            for step in range(i * PER_BANK, (i + 1) * PER_BANK):
                multiply(k, step)

        for k in range(2):
            for i in range(BANKS):
                multiply_bank(k, i)
        for i in range(LEAD):
            multiply_bank(2, i)
        for i in range(BANKS):
            if i >= LEAD:
                multiply_bank(2, i)
            multiply_bank(3, i)

        logits = held.tile([P, VB, N], F32, name="logits")
        for i in range(BANKS):
            for s in range(PER_BANK):
                step = i * PER_BANK + s
                bias_col = bias[:, s * BANKS + i : s * BANKS + i + 1]
                if i % 2 == 0:
                    nc.vector.tensor_scalar(logits[:, step, :], banks[i][:, s, :], bias_col, None, ADD)
                else:
                    nc.scalar.activation(logits[:, step, :], banks[i][:, s, :], IDENTITY, bias=bias_col)

        for i in range(BANKS):
            if i in (0, BANKS - 1):
                for s in range(PER_BANK):
                    nc.sync.dma_start(out_banks[:, i, s, :], logits[:, i * PER_BANK + s, :])
            else:
                nc.sync.dma_start(out_banks[:, i, :, :], logits[:, i * PER_BANK : (i + 1) * PER_BANK, :])
